import numpy as np
import ml_dtypes


def mxq(x, axis, fmt="e4m3"):
    dtype, down = {"e4m3": (ml_dtypes.float8_e4m3fn, 7), "e5m2": (ml_dtypes.float8_e5m2, 14)}[fmt]
    v = np.moveaxis(np.asarray(x, np.float32).astype(ml_dtypes.bfloat16).astype(np.float64), axis, -1)
    blocks = v.reshape(v.shape[:-1] + (-1, 32))
    amax = np.abs(blocks).max(-1, keepdims=True)
    byte = np.maximum(np.where(amax > 0, np.frexp(amax)[1] - 1 + 127, 0) - down, 1)
    scale = np.exp2(byte - 127.0)
    codes = (blocks / scale).astype(np.float32).astype(dtype).astype(np.float64)
    return np.moveaxis((codes * scale).reshape(v.shape), -1, axis)


WIDE = False


def mx_kscale(k):
    if not WIDE:
        return np.ones(k)
    levels = np.array([20, -20, 10, -10, 0])
    a = np.random.permutation(np.resize(levels, k // 512 * 4)).reshape(k // 512, 4)
    idx = np.arange(k)
    return np.exp2(a[idx // 512, idx % 128 // 32])


BF16 = ml_dtypes.bfloat16


def bf(x):
    return np.asarray(x, np.float32).astype(BF16)


def f64(x):
    return np.asarray(x).astype(np.float64)


B, I, O, G, P = 2048, 512, 512, 5, 3
GRID_RANGE = (-1.0, 1.0)
L = G + P


def make_grid():
    h = (GRID_RANGE[1] - GRID_RANGE[0]) / G
    n = G + 2 * P + 1
    return np.linspace(GRID_RANGE[0] - P * h, GRID_RANGE[1] + P * h, n)


def b_spline(x, grid, k):
    x = x[..., None]
    g = grid[None, None, :]
    basis = ((x >= g[..., :-1]) & (x < g[..., 1:])).astype(np.float64)
    for p in range(1, k + 1):
        left_denom = g[..., p:-1] - g[..., :-(p + 1)]
        right_denom = g[..., p + 1:] - g[..., 1:-p]
        left_denom = np.where(left_denom > 0, left_denom, np.ones_like(left_denom))
        right_denom = np.where(right_denom > 0, right_denom, np.ones_like(right_denom))
        left = (x - g[..., :-(p + 1)]) / left_denom * basis[..., :-1]
        right = (g[..., p + 1:] - x) / right_denom * basis[..., 1:]
        basis = left + right
    return basis


def d_b_spline(x, grid, k):
    low = b_spline(x, grid, k - 1)
    a = k / (grid[k:-1] - grid[:-(k + 1)])
    c = k / (grid[k + 1:] - grid[1:-k])
    return a * low[..., :-1] - c * low[..., 1:]


def setup_inputs():
    u = mx_kscale(O)
    x = np.random.uniform(-1.0, 1.0, (B, I))
    base_weight = np.random.uniform(-1.0, 1.0, (O, I)) * 3.0 / np.sqrt(I) / u[:, None]
    spline_weight = np.random.standard_normal((O, I, L)) * 1.5 / np.sqrt(I) / u[:, None, None]
    g = np.random.standard_normal((B, O)) * np.exp2(np.random.randint(-12, 1, (B, 1))) * 4.0 * u
    return {"x": bf(x), "base_weight": bf(base_weight), "spline_weight": bf(spline_weight), "grad_out": bf(g)}


def reference(x, base_weight, spline_weight, grad_out):
    x = f64(x)
    gq = mxq(f64(grad_out), 1, "e5m2")
    g_base = gq @ mxq(f64(base_weight), 0, "e4m3")
    g_basis = (gq @ mxq(f64(spline_weight).reshape(O, I * L), 0, "e4m3")).reshape(B, I, L)
    dbasis = d_b_spline(x, make_grid(), P)
    return g_base + (dbasis * g_basis).sum(axis=-1)

@@ -1,0 +1,172 @@
+from contextlib import ExitStack
+
+import concourse.bass as bass
+import concourse.mybir as mybir
+import concourse.tile as tile
+from concourse.masks import make_identity
+
+F32 = mybir.dt.float32
+BF16 = mybir.dt.bfloat16
+U32 = mybir.dt.uint32
+U8 = mybir.dt.uint8
+E4X4 = mybir.dt.float8_e4m3fn_x4
+E5X4 = mybir.dt.float8_e5m2_x4
+ALU = mybir.AluOpType
+ACT = mybir.ActivationFunctionType
+
+P = 128
+B, I, O, L = 2048, 512, 512, 8
+NT = B // P
+FLOPS = 2 * B * O * (I + I * L)
+
+H = 0.4
+XI = [-1.0 + H * k for k in range(6)]
+RS2 = 0.5 ** 0.5
+S = RS2 / H
+
+
+def tile_kanlayer_t_kernel(tc, x, base_weight, spline_weight, grad_out, out):
+    nc = tc.nc
+    with ExitStack() as ctx:
+        keep = ctx.enter_context(tc.tile_pool(name="keep", bufs=1))
+        pro = ctx.enter_context(tc.tile_pool(name="pro", bufs=1))
+        grp = ctx.enter_context(tc.tile_pool(name="grp", bufs=6))
+        plp = ctx.enter_context(tc.tile_pool(name="plp", bufs=2))
+        fnp = ctx.enter_context(tc.tile_pool(name="fnp", bufs=3))
+        outp = ctx.enter_context(tc.tile_pool(name="outp", bufs=3))
+        psum = ctx.enter_context(tc.psum_pool(name="psum", bufs=1))
+
+        ident = keep.tile([P, P], F32)
+        make_identity(nc, ident[:])
+        w_codes = keep.tile([P, L + 1, I], U32, align_bytes=64)
+        w_scales = keep.tile([P, L + 1, I], U8, align_bytes=64)
+        g_codes = keep.tile([P, 2, B], U32, align_bytes=64)
+        g_scales = keep.tile([P, 2, B], U8, align_bytes=64)
+        x_sb = keep.tile([P, NT, I], BF16)
+
+        g_sb = pro.tile([P, NT, O], BF16)
+        w_raw = pro.tile([P, 4, I * L], BF16)
+        wb_raw = pro.tile([P, 4, I], BF16)
+
+        g_view = grad_out.rearrange("(n p) o -> p n o", p=P)
+        x_view = x.rearrange("(n p) i -> p n i", p=P)
+        sw = spline_weight.rearrange("o i l -> o (i l)")
+        for q in range(4):
+            nc.sync.dma_start(out=g_sb[:, 4 * q : 4 * q + 4, :], in_=g_view[:, 4 * q : 4 * q + 4, :])
+        nc.sync.dma_start(out=x_sb[:, 0:4, :], in_=x_view[:, 0:4, :])
+        half = I * L // 2
+        for hf in range(2):
+            for u in range(2):
+                nc.sync.dma_start(
+                    out=w_raw[:, 2 * u : 2 * u + 2, hf * half : (hf + 1) * half],
+                    in_=sw[256 * u : 256 * u + 256, hf * half : (hf + 1) * half].rearrange("(q e) c -> q e c", e=2),
+                )
+        for u in range(2):
+            nc.sync.dma_start(
+                out=wb_raw[:, 2 * u : 2 * u + 2, :],
+                in_=base_weight[256 * u : 256 * u + 256, :].rearrange("(q e) c -> q e c", e=2),
+            )
+        for q in range(1, 4):
+            nc.sync.dma_start(out=x_sb[:, 4 * q : 4 * q + 4, :], in_=x_view[:, 4 * q : 4 * q + 4, :])
+
+        for q in range(4):
+            gg = grp.tile([P, 512, 4], BF16, align_bytes=64, tag="grouped", name="gg")
+            ggf = gg[:].rearrange("p b t -> p (b t)").bitcast(F32).rearrange("p (b u) -> p b u", u=2)
+            for c2 in range(2):
+                c = 2 * q + c2
+                xt = psum.tile([P, 2, 2, P], F32, tag="bank%d" % c, name="xt")
+                for n2 in range(2):
+                    n = 2 * c + n2
+                    gw = g_sb[:, n, :].bitcast(F32)
+                    for u in range(2):
+                        nc.tensor.transpose(xt[:, n2, u, :], gw[:, P * u : P * u + P], ident[:])
+                dst = ggf[:, 256 * c2 : 256 * c2 + 256, :].rearrange("p (n b) u -> p n b u", n=2)
+                src = xt[:].rearrange("p n u b -> p n b u")
+                if c2 == 0:
+                    nc.vector.tensor_copy(out=dst, in_=src)
+                else:
+                    nc.scalar.copy(out=dst, in_=src)
+            gg2 = grp.tile([P, 512, 4], BF16, align_bytes=64, tag="grouped", name="gg2")
+            flat = gg[:].rearrange("p b t -> p (b t)")
+            flat2 = gg2[:].rearrange("p b t -> p (b t)")
+            nc.vector.tensor_scalar(out=flat2, in0=flat, scalar1=-2.0, scalar2=None, op0=ALU.mult)
+            cols = slice(512 * q, 512 * q + 512)
+            nc.vector.quantize_mx(out=g_codes[:, 0, cols].bitcast(E5X4), scales=g_scales[:, 0, cols], in_=flat)
+            nc.vector.quantize_mx(out=g_codes[:, 1, cols].bitcast(E5X4), scales=g_scales[:, 1, cols], in_=flat2)
+
+        w_planes = w_raw[:].rearrange("p t (i l) -> p l i t", l=L)
+        for l in range(L + 1):
+            wg = grp.tile([P, 512, 4], BF16, align_bytes=64, tag="grouped", name="wg")
+            src = w_planes[:, l] if l < L else wb_raw[:].rearrange("p t i -> p i t")
+            if l % 2 == 0:
+                nc.vector.tensor_copy(out=wg[:], in_=src)
+            else:
+                nc.scalar.copy(out=wg[:], in_=src)
+            nc.vector.quantize_mx(
+                out=w_codes[:, l, :].bitcast(E4X4), scales=w_scales[:, l, :], in_=wg[:].rearrange("p i t -> p (i t)")
+            )
+
+        def mx(bank, n, v, l, start, stop):
+            cols = slice(P * n, P * n + P)
+            nc.tensor.matmul_mx(
+                out=bank[:],
+                lhsT=g_codes[:, v, cols].bitcast(E5X4),
+                lhsT_scale=g_scales[:, v, cols],
+                rhs=w_codes[:, l, :].bitcast(E4X4),
+                rhs_scale=w_scales[:, l, :],
+                start=start,
+                stop=stop,
+            )
+
+        for n in range(NT):
+            xs = x_sb[:, n, :]
+            pl = plp.tile([P, 5, I], F32)
+            fn = fnp.tile([P, 10, I], F32)
+            nc.scalar.activation(out=pl[:, 0, :], in_=xs, func=ACT.Relu, scale=-1.0 / H, bias=XI[1] / H)
+            nc.scalar.activation(out=pl[:, 4, :], in_=xs, func=ACT.Relu, scale=1.0 / H, bias=-XI[4] / H)
+            for k in range(1, 4):
+                nc.vector.tensor_scalar(
+                    out=pl[:, k, :], in0=xs, scalar1=XI[k], scalar2=XI[k + 1], op0=ALU.max, op1=ALU.min
+                )
+            nc.scalar.activation(out=fn[:, 0, :], in_=pl[:, 0, :], func=ACT.Square, scale=RS2, bias=0.0)
+            nc.scalar.activation(out=fn[:, 1, :], in_=pl[:, 0, :], func=ACT.Square, scale=-RS2, bias=RS2)
+            for k in range(1, 4):
+                nc.scalar.activation(out=fn[:, k + 1, :], in_=pl[:, k, :], func=ACT.Square, scale=S, bias=-S * XI[k])
+                nc.scalar.activation(out=fn[:, k + 5, :], in_=pl[:, k, :], func=ACT.Square, scale=-S, bias=S * XI[k + 1])
+            nc.scalar.activation(out=fn[:, 5, :], in_=pl[:, 4, :], func=ACT.Square, scale=RS2, bias=0.0)
+            nc.scalar.activation(out=fn[:, 9, :], in_=pl[:, 4, :], func=ACT.Square, scale=-RS2, bias=RS2)
+            nc.gpsimd.tensor_tensor(out=fn[:, 1:5, :], in0=fn[:, 1:5, :], in1=fn[:, 6:10, :], op=ALU.subtract)
+
+            banks = []
+            for m in range(1, 7):
+                hb = psum.tile([P, I], F32, tag="bank%d" % (m - 1), name="hb")
+                mx(hb, n, 0, m + 1, True, False)
+                mx(hb, n, 1, m, False, False)
+                mx(hb, n, 0, m - 1, False, True)
+                banks.append(hb)
+            cb = psum.tile([P, I], F32, tag="bank6", name="cb")
+            mx(cb, n, 0, 2, True, False)
+            mx(cb, n, 0, 2, False, False)
+            mx(cb, n, 1, 0, False, True)
+            gb = psum.tile([P, I], F32, tag="bank7", name="gb")
+            mx(gb, n, 0, L, True, True)
+
+            nc.vector.scalar_tensor_tensor(
+                out=fn[:, 0, :], in0=fn[:, 0, :], scalar=-0.5, in1=banks[0][:], op0=ALU.add, op1=ALU.mult
+            )
+            for m in range(2, 6):
+                nc.vector.scalar_tensor_tensor(
+                    out=fn[:, m - 1, :], in0=fn[:, m - 1, :], scalar=0.5, in1=banks[m - 1][:], op0=ALU.add, op1=ALU.mult
+                )
+            nc.vector.tensor_tensor(out=fn[:, 5, :], in0=fn[:, 5, :], in1=banks[5][:], op=ALU.mult)
+            nc.vector.scalar_tensor_tensor(
+                out=fn[:, 0, :], in0=cb[:], scalar=0.25, in1=fn[:, 0, :], op0=ALU.mult, op1=ALU.subtract
+            )
+            nc.vector.tensor_tensor(out=fn[:, 0:3, :], in0=fn[:, 0:3, :], in1=fn[:, 3:6, :], op=ALU.add)
+            nc.vector.tensor_tensor(out=fn[:, 0, :], in0=fn[:, 0, :], in1=fn[:, 1, :], op=ALU.add)
+            nc.vector.tensor_tensor(out=fn[:, 0, :], in0=fn[:, 0, :], in1=fn[:, 2, :], op=ALU.add)
+            ot = outp.tile([P, I], F32)
+            nc.vector.scalar_tensor_tensor(
+                out=ot[:], in0=fn[:, 0, :], scalar=2.5, in1=gb[:], op0=ALU.mult, op1=ALU.add
+            )
+            nc.sync.dma_start(out=out[P * n : P * n + P, :], in_=ot[:])

@@ -135,7 +135,7 @@ def tile_kanlayer_t_kernel(tc, x, base_weight, spline_weight, grad_out, out):
                 nc.scalar.activation(out=fn[:, k + 5, :], in_=pl[:, k, :], func=ACT.Square, scale=-S, bias=S * XI[k + 1])
             nc.scalar.activation(out=fn[:, 5, :], in_=pl[:, 4, :], func=ACT.Square, scale=RS2, bias=0.0)
             nc.scalar.activation(out=fn[:, 9, :], in_=pl[:, 4, :], func=ACT.Square, scale=-RS2, bias=RS2)
-            nc.gpsimd.tensor_tensor(out=fn[:, 1:5, :], in0=fn[:, 1:5, :], in1=fn[:, 6:10, :], op=ALU.subtract)
+            nc.vector.tensor_tensor(out=fn[:, 1:5, :], in0=fn[:, 1:5, :], in1=fn[:, 6:10, :], op=ALU.subtract)
 
             banks = []
             for m in range(1, 7):

@@ -1,8 +1,6 @@
 from contextlib import ExitStack
 
-import concourse.bass as bass
 import concourse.mybir as mybir
-import concourse.tile as tile
 from concourse.masks import make_identity
 
 F32 = mybir.dt.float32
@@ -16,157 +14,269 @@ ACT = mybir.ActivationFunctionType
 
 P = 128
 B, I, O, L = 2048, 512, 512, 8
-NT = B // P
 FLOPS = 2 * B * O * (I + I * L)
 
 H = 0.4
 XI = [-1.0 + H * k for k in range(6)]
-RS2 = 0.5 ** 0.5
-S = RS2 / H
+A = 1.25 ** 0.5
+S = A / H
+NTILES = 16
+NPLANES = 8
+LEAD = 6
 
 
 def tile_kanlayer_t_kernel(tc, x, base_weight, spline_weight, grad_out, out):
     nc = tc.nc
     with ExitStack() as ctx:
         keep = ctx.enter_context(tc.tile_pool(name="keep", bufs=1))
-        pro = ctx.enter_context(tc.tile_pool(name="pro", bufs=1))
-        grp = ctx.enter_context(tc.tile_pool(name="grp", bufs=6))
+        grp = ctx.enter_context(tc.tile_pool(name="grp", bufs=2))
         plp = ctx.enter_context(tc.tile_pool(name="plp", bufs=2))
         fnp = ctx.enter_context(tc.tile_pool(name="fnp", bufs=3))
+        fbp = ctx.enter_context(tc.tile_pool(name="fbp", bufs=2))
         outp = ctx.enter_context(tc.tile_pool(name="outp", bufs=3))
-        psum = ctx.enter_context(tc.psum_pool(name="psum", bufs=1))
+        psum = ctx.enter_context(tc.psum_pool(name="psum", bufs=LEAD))
+        aux = ctx.enter_context(tc.psum_pool(name="aux", bufs=2))
+        ctx.enter_context(tc.manual_schedule())
 
         ident = keep.tile([P, P], F32)
         make_identity(nc, ident[:])
-        w_codes = keep.tile([P, L + 1, I], U32, align_bytes=64)
-        w_scales = keep.tile([P, L + 1, I], U8, align_bytes=64)
+        ident_bf = keep.tile([P, P], BF16)
+        make_identity(nc, ident_bf[:])
+        w_codes = keep.tile([P, 4, L, P], U32, align_bytes=64)
+        w_scales = keep.tile([P, 4, L, P], U8, align_bytes=64)
+        wb_codes = keep.tile([P, I], U32, align_bytes=64)
+        wb_scales = keep.tile([P, I], U8, align_bytes=64)
         g_codes = keep.tile([P, 2, B], U32, align_bytes=64)
         g_scales = keep.tile([P, 2, B], U8, align_bytes=64)
-        x_sb = keep.tile([P, NT, I], BF16)
-
-        g_sb = pro.tile([P, NT, O], BF16)
-        w_raw = pro.tile([P, 4, I * L], BF16)
-        wb_raw = pro.tile([P, 4, I], BF16)
+        xT = keep.tile([P, 4, B], BF16)
+        x_sb = keep.tile([P, 16, I], BF16)
+        g_sb = keep.tile([P, 16, O], BF16)
+        w_raw = keep.tile([P, 4, 4, L * P], BF16)
+        wb_raw = keep.tile([P, 4, I], BF16)
+        wg = keep.tile([P, L, P, 4], BF16, align_bytes=64)
 
         g_view = grad_out.rearrange("(n p) o -> p n o", p=P)
         x_view = x.rearrange("(n p) i -> p n i", p=P)
         sw = spline_weight.rearrange("o i l -> o (i l)")
-        for q in range(4):
-            nc.sync.dma_start(out=g_sb[:, 4 * q : 4 * q + 4, :], in_=g_view[:, 4 * q : 4 * q + 4, :])
-        nc.sync.dma_start(out=x_sb[:, 0:4, :], in_=x_view[:, 0:4, :])
-        half = I * L // 2
-        for hf in range(2):
+
+        def load_g(bc):
+            nc.sync.dma_start(out=g_sb[:, 4 * bc : 4 * bc + 4, :], in_=g_view[:, 4 * bc : 4 * bc + 4, :])
+
+        def load_x(bc):
+            nc.sync.dma_start(out=x_sb[:, 4 * bc : 4 * bc + 4, :], in_=x_view[:, 4 * bc : 4 * bc + 4, :])
+
+        def load_w(j):
             for u in range(2):
                 nc.sync.dma_start(
-                    out=w_raw[:, 2 * u : 2 * u + 2, hf * half : (hf + 1) * half],
-                    in_=sw[256 * u : 256 * u + 256, hf * half : (hf + 1) * half].rearrange("(q e) c -> q e c", e=2),
+                    out=w_raw[:, j, 2 * u : 2 * u + 2, :],
+                    in_=sw[256 * u : 256 * u + 256, L * P * j : L * P * (j + 1)].rearrange("(q e) c -> q e c", e=2),
                 )
+
+        load_g(0)
+        load_w(0)
+        load_x(0)
         for u in range(2):
             nc.sync.dma_start(
                 out=wb_raw[:, 2 * u : 2 * u + 2, :],
                 in_=base_weight[256 * u : 256 * u + 256, :].rearrange("(q e) c -> q e c", e=2),
             )
-        for q in range(1, 4):
-            nc.sync.dma_start(out=x_sb[:, 4 * q : 4 * q + 4, :], in_=x_view[:, 4 * q : 4 * q + 4, :])
+        for bc in range(1, 4):
+            load_g(bc)
+            load_x(bc)
+        for j in range(1, 4):
+            load_w(j)
 
-        for q in range(4):
-            gg = grp.tile([P, 512, 4], BF16, align_bytes=64, tag="grouped", name="gg")
+        def pre_g(bc):
+            gg = grp.tile([P, 512, 4], BF16, align_bytes=64, tag="gg", name="gg")
             ggf = gg[:].rearrange("p b t -> p (b t)").bitcast(F32).rearrange("p (b u) -> p b u", u=2)
             for c2 in range(2):
-                c = 2 * q + c2
-                xt = psum.tile([P, 2, 2, P], F32, tag="bank%d" % c, name="xt")
+                xt = aux.tile([P, 2, 2, P], F32, tag="aux", name="xt")
                 for n2 in range(2):
-                    n = 2 * c + n2
-                    gw = g_sb[:, n, :].bitcast(F32)
+                    gw = g_sb[:, 4 * bc + 2 * c2 + n2, :].bitcast(F32)
                     for u in range(2):
                         nc.tensor.transpose(xt[:, n2, u, :], gw[:, P * u : P * u + P], ident[:])
-                dst = ggf[:, 256 * c2 : 256 * c2 + 256, :].rearrange("p (n b) u -> p n b u", n=2)
-                src = xt[:].rearrange("p n u b -> p n b u")
-                if c2 == 0:
-                    nc.vector.tensor_copy(out=dst, in_=src)
-                else:
-                    nc.scalar.copy(out=dst, in_=src)
-            gg2 = grp.tile([P, 512, 4], BF16, align_bytes=64, tag="grouped", name="gg2")
+                nc.scalar.copy(
+                    out=ggf[:, 256 * c2 : 256 * c2 + 256, :].rearrange("p (n b) u -> p n b u", n=2),
+                    in_=xt[:].rearrange("p n u b -> p n b u"),
+                )
+            gg2 = grp.tile([P, 512, 4], BF16, align_bytes=64, tag="gg2", name="gg2")
             flat = gg[:].rearrange("p b t -> p (b t)")
             flat2 = gg2[:].rearrange("p b t -> p (b t)")
             nc.vector.tensor_scalar(out=flat2, in0=flat, scalar1=-2.0, scalar2=None, op0=ALU.mult)
-            cols = slice(512 * q, 512 * q + 512)
+            cols = slice(512 * bc, 512 * bc + 512)
             nc.vector.quantize_mx(out=g_codes[:, 0, cols].bitcast(E5X4), scales=g_scales[:, 0, cols], in_=flat)
             nc.vector.quantize_mx(out=g_codes[:, 1, cols].bitcast(E5X4), scales=g_scales[:, 1, cols], in_=flat2)
 
-        w_planes = w_raw[:].rearrange("p t (i l) -> p l i t", l=L)
-        for l in range(L + 1):
-            wg = grp.tile([P, 512, 4], BF16, align_bytes=64, tag="grouped", name="wg")
-            src = w_planes[:, l] if l < L else wb_raw[:].rearrange("p t i -> p i t")
-            if l % 2 == 0:
-                nc.vector.tensor_copy(out=wg[:], in_=src)
-            else:
-                nc.scalar.copy(out=wg[:], in_=src)
+        def pre_x(bc):
+            for j2 in range(2):
+                xp = aux.tile([P, 2, 512], BF16, tag="aux", name="xp")
+                for jj in range(2):
+                    j = 2 * j2 + jj
+                    for q in range(4):
+                        nc.tensor.transpose(
+                            xp[:, jj, P * q : P * q + P], x_sb[:, 4 * bc + q, P * j : P * j + P], ident_bf[:]
+                        )
+                nc.scalar.copy(out=xT[:, 2 * j2 : 2 * j2 + 2, 512 * bc : 512 * bc + 512], in_=xp[:])
+
+        def pre_w(j):
+            src = w_raw[:, j].rearrange("p t (i l) -> p l i t", l=L)
+            nc.vector.tensor_copy(out=wg[:, 0:4], in_=src[:, 0:4])
+            nc.scalar.copy(out=wg[:, 4:8], in_=src[:, 4:8])
             nc.vector.quantize_mx(
-                out=w_codes[:, l, :].bitcast(E4X4), scales=w_scales[:, l, :], in_=wg[:].rearrange("p i t -> p (i t)")
+                out=w_codes[:, j].rearrange("p l i -> p (l i)").bitcast(E4X4),
+                scales=w_scales[:, j].rearrange("p l i -> p (l i)"),
+                in_=wg[:].rearrange("p l i t -> p (l i t)"),
             )
 
-        def mx(bank, n, v, l, start, stop):
-            cols = slice(P * n, P * n + P)
-            nc.tensor.matmul_mx(
-                out=bank[:],
-                lhsT=g_codes[:, v, cols].bitcast(E5X4),
-                lhsT_scale=g_scales[:, v, cols],
-                rhs=w_codes[:, l, :].bitcast(E4X4),
-                rhs_scale=w_scales[:, l, :],
-                start=start,
-                stop=stop,
+        def pre_base():
+            wbg = grp.tile([P, 512, 4], BF16, align_bytes=64, tag="gg", name="wbg")
+            nc.vector.tensor_copy(out=wbg[:], in_=wb_raw[:].rearrange("p t i -> p i t"))
+            nc.vector.quantize_mx(
+                out=wb_codes[:].bitcast(E4X4), scales=wb_scales[:], in_=wbg[:].rearrange("p i t -> p (i t)")
             )
 
-        for n in range(NT):
-            xs = x_sb[:, n, :]
-            pl = plp.tile([P, 5, I], F32)
-            fn = fnp.tile([P, 10, I], F32)
-            nc.scalar.activation(out=pl[:, 0, :], in_=xs, func=ACT.Relu, scale=-1.0 / H, bias=XI[1] / H)
-            nc.scalar.activation(out=pl[:, 4, :], in_=xs, func=ACT.Relu, scale=1.0 / H, bias=-XI[4] / H)
+        fns = {}
+        fbs = {}
+        pls = {}
+        banks = {}
+        obs = {}
+
+        def func_v(t):
+            j, bc = t // 4, t % 4
+            xs = xT[:, j, 512 * bc : 512 * bc + 512]
+            pl = plp.tile([P, 5, 512], F32, name="pl")
+            pls[t] = pl
             for k in range(1, 4):
                 nc.vector.tensor_scalar(
                     out=pl[:, k, :], in0=xs, scalar1=XI[k], scalar2=XI[k + 1], op0=ALU.max, op1=ALU.min
                 )
-            nc.scalar.activation(out=fn[:, 0, :], in_=pl[:, 0, :], func=ACT.Square, scale=RS2, bias=0.0)
-            nc.scalar.activation(out=fn[:, 1, :], in_=pl[:, 0, :], func=ACT.Square, scale=-RS2, bias=RS2)
+
+        def func_s_head(t):
+            j, bc = t // 4, t % 4
+            xs = xT[:, j, 512 * bc : 512 * bc + 512]
+            pl = pls[t]
+            fn = fnp.tile([P, 6, 512], F32, name="fn")
+            fb = fbp.tile([P, 4, 512], F32, name="fb")
+            fns[t] = fn
+            fbs[t] = fb
+            nc.scalar.activation(out=pl[:, 0, :], in_=xs, func=ACT.Relu, scale=-1.0 / H, bias=XI[1] / H)
+            nc.scalar.activation(out=pl[:, 4, :], in_=xs, func=ACT.Relu, scale=1.0 / H, bias=-XI[4] / H)
+            nc.scalar.activation(out=fn[:, 0, :], in_=pl[:, 0, :], func=ACT.Square, scale=A, bias=0.0)
+            nc.scalar.activation(out=fn[:, 1, :], in_=pl[:, 0, :], func=ACT.Square, scale=-A, bias=A)
+
+        def func_s_tail(t):
+            pl, fn, fb = pls[t], fns[t], fbs[t]
             for k in range(1, 4):
                 nc.scalar.activation(out=fn[:, k + 1, :], in_=pl[:, k, :], func=ACT.Square, scale=S, bias=-S * XI[k])
-                nc.scalar.activation(out=fn[:, k + 5, :], in_=pl[:, k, :], func=ACT.Square, scale=-S, bias=S * XI[k + 1])
-            nc.scalar.activation(out=fn[:, 5, :], in_=pl[:, 4, :], func=ACT.Square, scale=RS2, bias=0.0)
-            nc.scalar.activation(out=fn[:, 9, :], in_=pl[:, 4, :], func=ACT.Square, scale=-RS2, bias=RS2)
-            nc.vector.tensor_tensor(out=fn[:, 1:5, :], in0=fn[:, 1:5, :], in1=fn[:, 6:10, :], op=ALU.subtract)
+                nc.scalar.activation(out=fb[:, k - 1, :], in_=pl[:, k, :], func=ACT.Square, scale=-S, bias=S * XI[k + 1])
+            nc.scalar.activation(out=fn[:, 5, :], in_=pl[:, 4, :], func=ACT.Square, scale=A, bias=0.0)
+            nc.scalar.activation(out=fb[:, 3, :], in_=pl[:, 4, :], func=ACT.Square, scale=-A, bias=A)
 
-            banks = []
-            for m in range(1, 7):
-                hb = psum.tile([P, I], F32, tag="bank%d" % (m - 1), name="hb")
-                mx(hb, n, 0, m + 1, True, False)
-                mx(hb, n, 1, m, False, False)
-                mx(hb, n, 0, m - 1, False, True)
-                banks.append(hb)
-            cb = psum.tile([P, I], F32, tag="bank6", name="cb")
-            mx(cb, n, 0, 2, True, False)
-            mx(cb, n, 0, 2, False, False)
-            mx(cb, n, 1, 0, False, True)
-            gb = psum.tile([P, I], F32, tag="bank7", name="gb")
-            mx(gb, n, 0, L, True, True)
-
-            nc.vector.scalar_tensor_tensor(
-                out=fn[:, 0, :], in0=fn[:, 0, :], scalar=-0.5, in1=banks[0][:], op0=ALU.add, op1=ALU.mult
+        def mx(bank, j, bc, v, l, start, stop):
+            gc = slice(512 * bc, 512 * bc + 512)
+            if l < L:
+                lhsT, lhsT_scale = w_codes[:, j, l, :], w_scales[:, j, l, :]
+            else:
+                lhsT, lhsT_scale = wb_codes[:, P * j : P * j + P], wb_scales[:, P * j : P * j + P]
+            nc.tensor.matmul_mx(
+                out=bank[:],
+                lhsT=lhsT.bitcast(E4X4),
+                lhsT_scale=lhsT_scale,
+                rhs=g_codes[:, v, gc].bitcast(E5X4),
+                rhs_scale=g_scales[:, v, gc],
+                start=start,
+                stop=stop,
             )
-            for m in range(2, 6):
+
+        def issue_mx(q):
+            t, p = q // NPLANES, q % NPLANES
+            j, bc = t // 4, t % 4
+            bank = psum.tile([P, 512], F32, tag="mx", name="bank")
+            banks[q] = bank
+            if p < 6:
+                mx(bank, j, bc, 0, p + 2, True, False)
+                mx(bank, j, bc, 1, p + 1, False, False)
+                mx(bank, j, bc, 0, p, False, True)
+            elif p == 6:
+                mx(bank, j, bc, 0, 2, True, False)
+                mx(bank, j, bc, 0, 2, False, False)
+                mx(bank, j, bc, 1, 0, False, True)
+            else:
+                mx(bank, j, bc, 0, L, True, True)
+
+        def consume(q):
+            t, p = q // NPLANES, q % NPLANES
+            fn = fns[t]
+            bank = banks[q]
+            if p == 0:
                 nc.vector.scalar_tensor_tensor(
-                    out=fn[:, m - 1, :], in0=fn[:, m - 1, :], scalar=0.5, in1=banks[m - 1][:], op0=ALU.add, op1=ALU.mult
+                    out=fn[:, 0, :], in0=fn[:, 0, :], scalar=-1.25, in1=bank[:], op0=ALU.add, op1=ALU.mult
                 )
-            nc.vector.tensor_tensor(out=fn[:, 5, :], in0=fn[:, 5, :], in1=banks[5][:], op=ALU.mult)
-            nc.vector.scalar_tensor_tensor(
-                out=fn[:, 0, :], in0=cb[:], scalar=0.25, in1=fn[:, 0, :], op0=ALU.mult, op1=ALU.subtract
+            elif p < 5:
+                nc.vector.scalar_tensor_tensor(
+                    out=fn[:, p, :], in0=fn[:, p, :], scalar=1.25, in1=bank[:], op0=ALU.add, op1=ALU.mult
+                )
+            elif p == 5:
+                nc.vector.tensor_tensor(out=fn[:, 5, :], in0=fn[:, 5, :], in1=bank[:], op=ALU.mult)
+            elif p == 6:
+                nc.vector.scalar_tensor_tensor(
+                    out=fn[:, 0, :], in0=bank[:], scalar=0.625, in1=fn[:, 0, :], op0=ALU.mult, op1=ALU.subtract
+                )
+            else:
+                nc.vector.tensor_tensor(out=fn[:, 1, :], in0=fn[:, 1, :], in1=bank[:], op=ALU.add)
+
+        def adder(t):
+            fn = fns[t]
+            ob = aux.tile([P, 4, P], F32, tag="aux", name="ob")
+            obs[t] = ob
+            for r in range(4):
+                for a in range(6):
+                    nc.tensor.matmul(
+                        out=ob[:, r, :],
+                        lhsT=fn[:, a, P * r : P * r + P],
+                        rhs=ident[:],
+                        is_transpose=True,
+                        start=(a == 0),
+                        stop=(a == 5),
+                    )
+
+        def finish(t):
+            j, bc = t // 4, t % 4
+            ot = outp.tile([P, 4, P], F32, name="ot")
+            nc.scalar.copy(out=ot[:], in_=obs[t][:])
+            nc.sync.dma_start(
+                out=out[512 * bc : 512 * bc + 512, P * j : P * j + P].rearrange("(r p) i -> p r i", p=P), in_=ot[:]
             )
-            nc.vector.tensor_tensor(out=fn[:, 0:3, :], in0=fn[:, 0:3, :], in1=fn[:, 3:6, :], op=ALU.add)
-            nc.vector.tensor_tensor(out=fn[:, 0, :], in0=fn[:, 0, :], in1=fn[:, 1, :], op=ALU.add)
-            nc.vector.tensor_tensor(out=fn[:, 0, :], in0=fn[:, 0, :], in1=fn[:, 2, :], op=ALU.add)
-            ot = outp.tile([P, I], F32)
-            nc.vector.scalar_tensor_tensor(
-                out=ot[:], in0=fn[:, 0, :], scalar=2.5, in1=gb[:], op0=ALU.mult, op1=ALU.add
-            )
-            nc.sync.dma_start(out=out[P * n : P * n + P, :], in_=ot[:])
+
+        pre_g(0)
+        pre_w(0)
+        pre_x(0)
+        func_v(0)
+        func_s_head(0)
+        func_s_tail(0)
+        pre_base()
+        for q in range(LEAD):
+            issue_mx(q)
+        pre_g(1)
+        pre_x(1)
+        for t in range(NTILES):
+            if t + 1 < NTILES:
+                func_v(t + 1)
+                func_s_head(t + 1)
+            if t >= 1:
+                finish(t - 1)
+            if t + 1 < NTILES:
+                func_s_tail(t + 1)
+            nc.vector.tensor_tensor(out=fns[t][:, 1:5, :], in0=fns[t][:, 1:5, :], in1=fbs[t][:], op=ALU.subtract)
+            for p in range(NPLANES):
+                q = NPLANES * t + p
+                consume(q)
+                if q + LEAD < NPLANES * NTILES:
+                    issue_mx(q + LEAD)
+            adder(t)
+            if t + 2 < 4:
+                pre_g(t + 2)
+                pre_x(t + 2)
+            if t % 4 == 1 and t // 4 + 1 < 4:
+                pre_w(t // 4 + 1)
+        finish(NTILES - 1)

@@ -72,56 +72,76 @@ def tile_kanlayer_t_kernel(tc, x, base_weight, spline_weight, grad_out, out):
                     in_=sw[256 * u : 256 * u + 256, L * P * j : L * P * (j + 1)].rearrange("(q e) c -> q e c", e=2),
                 )
 
+        load_x(0)
         load_g(0)
         load_w(0)
-        load_x(0)
+        load_g(1)
+        load_x(1)
         for u in range(2):
             nc.sync.dma_start(
                 out=wb_raw[:, 2 * u : 2 * u + 2, :],
                 in_=base_weight[256 * u : 256 * u + 256, :].rearrange("(q e) c -> q e c", e=2),
             )
-        for bc in range(1, 4):
+        for bc in range(2, 4):
             load_g(bc)
             load_x(bc)
         for j in range(1, 4):
             load_w(j)
 
-        def pre_g(bc):
-            gg = grp.tile([P, 512, 4], BF16, align_bytes=64, tag="gg", name="gg")
-            ggf = gg[:].rearrange("p b t -> p (b t)").bitcast(F32).rearrange("p (b u) -> p b u", u=2)
-            for c2 in range(2):
-                xt = aux.tile([P, 2, 2, P], F32, tag="aux", name="xt")
-                for n2 in range(2):
-                    gw = g_sb[:, 4 * bc + 2 * c2 + n2, :].bitcast(F32)
-                    for u in range(2):
-                        nc.tensor.transpose(xt[:, n2, u, :], gw[:, P * u : P * u + P], ident[:])
-                nc.scalar.copy(
-                    out=ggf[:, 256 * c2 : 256 * c2 + 256, :].rearrange("p (n b) u -> p n b u", n=2),
-                    in_=xt[:].rearrange("p n u b -> p n b u"),
-                )
+        ggs = {}
+        xts = {}
+        xps = {}
+
+        def g_transpose(bc, c2):
+            xt = aux.tile([P, 2, 2, P], F32, tag="aux", name="xt")
+            xts[(bc, c2)] = xt
+            for n2 in range(2):
+                gw = g_sb[:, 4 * bc + 2 * c2 + n2, :].bitcast(F32)
+                for u in range(2):
+                    nc.tensor.transpose(xt[:, n2, u, :], gw[:, P * u : P * u + P], ident[:])
+
+        def g_copy(bc, c2, on_vector):
+            if c2 == 0:
+                ggs[bc] = grp.tile([P, 512, 4], BF16, align_bytes=64, tag="gg", name="gg")
+            ggf = ggs[bc][:].rearrange("p b t -> p (b t)").bitcast(F32).rearrange("p (b u) -> p b u", u=2)
+            dst = ggf[:, 256 * c2 : 256 * c2 + 256, :].rearrange("p (n b) u -> p n b u", n=2)
+            src = xts[(bc, c2)][:].rearrange("p n u b -> p n b u")
+            if on_vector:
+                nc.vector.tensor_copy(out=dst, in_=src)
+            else:
+                nc.scalar.copy(out=dst, in_=src)
+
+        def g_quantise(bc):
             gg2 = grp.tile([P, 512, 4], BF16, align_bytes=64, tag="gg2", name="gg2")
-            flat = gg[:].rearrange("p b t -> p (b t)")
+            flat = ggs[bc][:].rearrange("p b t -> p (b t)")
             flat2 = gg2[:].rearrange("p b t -> p (b t)")
             nc.vector.tensor_scalar(out=flat2, in0=flat, scalar1=-2.0, scalar2=None, op0=ALU.mult)
             cols = slice(512 * bc, 512 * bc + 512)
             nc.vector.quantize_mx(out=g_codes[:, 0, cols].bitcast(E5X4), scales=g_scales[:, 0, cols], in_=flat)
             nc.vector.quantize_mx(out=g_codes[:, 1, cols].bitcast(E5X4), scales=g_scales[:, 1, cols], in_=flat2)
 
-        def pre_x(bc):
-            for j2 in range(2):
-                xp = aux.tile([P, 2, 512], BF16, tag="aux", name="xp")
-                for jj in range(2):
-                    j = 2 * j2 + jj
-                    for q in range(4):
-                        nc.tensor.transpose(
-                            xp[:, jj, P * q : P * q + P], x_sb[:, 4 * bc + q, P * j : P * j + P], ident_bf[:]
-                        )
-                nc.scalar.copy(out=xT[:, 2 * j2 : 2 * j2 + 2, 512 * bc : 512 * bc + 512], in_=xp[:])
+        def x_transpose(bc, j2):
+            xp = aux.tile([P, 2, 512], BF16, tag="aux", name="xp")
+            xps[(bc, j2)] = xp
+            for jj in range(2):
+                j = 2 * j2 + jj
+                for q in range(4):
+                    nc.tensor.transpose(
+                        xp[:, jj, P * q : P * q + P], x_sb[:, 4 * bc + q, P * j : P * j + P], ident_bf[:]
+                    )
 
-        def pre_w(j):
+        def x_copy(bc, j2):
+            nc.scalar.copy(out=xT[:, 2 * j2 : 2 * j2 + 2, 512 * bc : 512 * bc + 512], in_=xps[(bc, j2)][:])
+
+        def w_regroup(j, on_vector):
             src = w_raw[:, j].rearrange("p t (i l) -> p l i t", l=L)
-            nc.vector.tensor_copy(out=wg[:, 0:4], in_=src[:, 0:4])
-            nc.scalar.copy(out=wg[:, 4:8], in_=src[:, 4:8])
+            cut = 4 if j == 0 else 2
+            if on_vector:
+                nc.vector.tensor_copy(out=wg[:, 0:cut], in_=src[:, 0:cut])
+            else:
+                nc.scalar.copy(out=wg[:, cut:L], in_=src[:, cut:L])
+
+        def w_quantise(j):
             nc.vector.quantize_mx(
                 out=w_codes[:, j].rearrange("p l i -> p (l i)").bitcast(E4X4),
                 scales=w_scales[:, j].rearrange("p l i -> p (l i)"),
@@ -130,7 +150,7 @@ def tile_kanlayer_t_kernel(tc, x, base_weight, spline_weight, grad_out, out):
 
         def pre_base():
             wbg = grp.tile([P, 512, 4], BF16, align_bytes=64, tag="gg", name="wbg")
-            nc.vector.tensor_copy(out=wbg[:], in_=wb_raw[:].rearrange("p t i -> p i t"))
+            nc.scalar.copy(out=wbg[:], in_=wb_raw[:].rearrange("p t i -> p i t"))
             nc.vector.quantize_mx(
                 out=wb_codes[:].bitcast(E4X4), scales=wb_scales[:], in_=wbg[:].rearrange("p i t -> p (i t)")
             )
@@ -163,14 +183,14 @@ def tile_kanlayer_t_kernel(tc, x, base_weight, spline_weight, grad_out, out):
             nc.scalar.activation(out=pl[:, 4, :], in_=xs, func=ACT.Relu, scale=1.0 / H, bias=-XI[4] / H)
             nc.scalar.activation(out=fn[:, 0, :], in_=pl[:, 0, :], func=ACT.Square, scale=A, bias=0.0)
             nc.scalar.activation(out=fn[:, 1, :], in_=pl[:, 0, :], func=ACT.Square, scale=-A, bias=A)
+            nc.scalar.activation(out=fn[:, 5, :], in_=pl[:, 4, :], func=ACT.Square, scale=A, bias=0.0)
+            nc.scalar.activation(out=fb[:, 3, :], in_=pl[:, 4, :], func=ACT.Square, scale=-A, bias=A)
 
         def func_s_tail(t):
             pl, fn, fb = pls[t], fns[t], fbs[t]
             for k in range(1, 4):
                 nc.scalar.activation(out=fn[:, k + 1, :], in_=pl[:, k, :], func=ACT.Square, scale=S, bias=-S * XI[k])
                 nc.scalar.activation(out=fb[:, k - 1, :], in_=pl[:, k, :], func=ACT.Square, scale=-S, bias=S * XI[k + 1])
-            nc.scalar.activation(out=fn[:, 5, :], in_=pl[:, 4, :], func=ACT.Square, scale=A, bias=0.0)
-            nc.scalar.activation(out=fb[:, 3, :], in_=pl[:, 4, :], func=ACT.Square, scale=-A, bias=A)
 
         def mx(bank, j, bc, v, l, start, stop):
             gc = slice(512 * bc, 512 * bc + 512)
@@ -248,25 +268,53 @@ def tile_kanlayer_t_kernel(tc, x, base_weight, spline_weight, grad_out, out):
                 out=out[512 * bc : 512 * bc + 512, P * j : P * j + P].rearrange("(r p) i -> p r i", p=P), in_=ot[:]
             )
 
-        pre_g(0)
-        pre_w(0)
-        pre_x(0)
+        x_transpose(0, 0)
+        x_copy(0, 0)
+        g_transpose(0, 0)
+        g_transpose(0, 1)
+        g_copy(0, 0, False)
+        g_copy(0, 1, False)
         func_v(0)
         func_s_head(0)
+        g_quantise(0)
+        w_regroup(0, True)
+        w_regroup(0, False)
+        x_transpose(1, 0)
+        g_transpose(1, 0)
+        g_copy(1, 0, True)
+        g_transpose(1, 1)
+        g_copy(1, 1, True)
+        w_quantise(0)
         func_s_tail(0)
-        pre_base()
+        x_copy(1, 0)
         for q in range(LEAD):
             issue_mx(q)
-        pre_g(1)
-        pre_x(1)
+        g_quantise(1)
+        pre_base()
         for t in range(NTILES):
             if t + 1 < NTILES:
                 func_v(t + 1)
                 func_s_head(t + 1)
+                func_s_tail(t + 1)
             if t >= 1:
                 finish(t - 1)
-            if t + 1 < NTILES:
-                func_s_tail(t + 1)
+            if t + 2 < 4:
+                x_transpose(t + 2, 0)
+                g_transpose(t + 2, 0)
+                x_copy(t + 2, 0)
+                g_transpose(t + 2, 1)
+                g_copy(t + 2, 0, False)
+                g_copy(t + 2, 1, False)
+            if 2 <= t < 6:
+                x_transpose(t - 2, 1)
+                x_copy(t - 2, 1)
+            if t % 4 == 1 and t // 4 + 1 < 4:
+                w_regroup(t // 4 + 1, False)
+            if 2 <= t + 1 < 4:
+                g_quantise(t + 1)
+            if t % 4 == 2 and t // 4 + 1 < 4:
+                w_regroup(t // 4 + 1, True)
+                w_quantise(t // 4 + 1)
             nc.vector.tensor_tensor(out=fns[t][:, 1:5, :], in0=fns[t][:, 1:5, :], in1=fbs[t][:], op=ALU.subtract)
             for p in range(NPLANES):
                 q = NPLANES * t + p
@@ -274,9 +322,4 @@ def tile_kanlayer_t_kernel(tc, x, base_weight, spline_weight, grad_out, out):
                 if q + LEAD < NPLANES * NTILES:
                     issue_mx(q + LEAD)
             adder(t)
-            if t + 2 < 4:
-                pre_g(t + 2)
-                pre_x(t + 2)
-            if t % 4 == 1 and t // 4 + 1 < 4:
-                pre_w(t // 4 + 1)
         finish(NTILES - 1)

@@ -166,7 +166,7 @@ def tile_kanlayer_t_kernel(tc, x, base_weight, spline_weight, grad_out, out):
             xs = xT[:, j, 512 * bc : 512 * bc + 512]
             pl = plp.tile([P, 5, 512], F32, name="pl")
             pls[t] = pl
-            for k in range(1, 4):
+            for k in (0, 4, 1, 2, 3):
                 nc.vector.tensor_scalar(
                     out=pl[:, k, :], in0=xs, scalar1=XI[k], scalar2=XI[k + 1], op0=ALU.max, op1=ALU.min
                 )
@@ -179,12 +179,10 @@ def tile_kanlayer_t_kernel(tc, x, base_weight, spline_weight, grad_out, out):
             fb = fbp.tile([P, 4, 512], F32, name="fb")
             fns[t] = fn
             fbs[t] = fb
-            nc.scalar.activation(out=pl[:, 0, :], in_=xs, func=ACT.Relu, scale=-1.0 / H, bias=XI[1] / H)
-            nc.scalar.activation(out=pl[:, 4, :], in_=xs, func=ACT.Relu, scale=1.0 / H, bias=-XI[4] / H)
-            nc.scalar.activation(out=fn[:, 0, :], in_=pl[:, 0, :], func=ACT.Square, scale=A, bias=0.0)
-            nc.scalar.activation(out=fn[:, 1, :], in_=pl[:, 0, :], func=ACT.Square, scale=-A, bias=A)
-            nc.scalar.activation(out=fn[:, 5, :], in_=pl[:, 4, :], func=ACT.Square, scale=A, bias=0.0)
-            nc.scalar.activation(out=fb[:, 3, :], in_=pl[:, 4, :], func=ACT.Square, scale=-A, bias=A)
+            nc.scalar.activation(out=fn[:, 0, :], in_=pl[:, 0, :], func=ACT.Square, scale=-S, bias=S * XI[1])
+            nc.scalar.activation(out=fn[:, 1, :], in_=pl[:, 0, :], func=ACT.Square, scale=S, bias=-S * XI[0])
+            nc.scalar.activation(out=fn[:, 5, :], in_=pl[:, 4, :], func=ACT.Square, scale=S, bias=-S * XI[4])
+            nc.scalar.activation(out=fb[:, 3, :], in_=pl[:, 4, :], func=ACT.Square, scale=-S, bias=S * XI[5])
 
         def func_s_tail(t):
             pl, fn, fb = pls[t], fns[t], fbs[t]

@@ -166,7 +166,7 @@ def tile_kanlayer_t_kernel(tc, x, base_weight, spline_weight, grad_out, out):
             xs = xT[:, j, 512 * bc : 512 * bc + 512]
             pl = plp.tile([P, 5, 512], F32, name="pl")
             pls[t] = pl
-            for k in (0, 4, 1, 2, 3):
+            for k in range(1, 4):
                 nc.vector.tensor_scalar(
                     out=pl[:, k, :], in0=xs, scalar1=XI[k], scalar2=XI[k + 1], op0=ALU.max, op1=ALU.min
                 )
@@ -179,10 +179,12 @@ def tile_kanlayer_t_kernel(tc, x, base_weight, spline_weight, grad_out, out):
             fb = fbp.tile([P, 4, 512], F32, name="fb")
             fns[t] = fn
             fbs[t] = fb
-            nc.scalar.activation(out=fn[:, 0, :], in_=pl[:, 0, :], func=ACT.Square, scale=-S, bias=S * XI[1])
-            nc.scalar.activation(out=fn[:, 1, :], in_=pl[:, 0, :], func=ACT.Square, scale=S, bias=-S * XI[0])
-            nc.scalar.activation(out=fn[:, 5, :], in_=pl[:, 4, :], func=ACT.Square, scale=S, bias=-S * XI[4])
-            nc.scalar.activation(out=fb[:, 3, :], in_=pl[:, 4, :], func=ACT.Square, scale=-S, bias=S * XI[5])
+            nc.scalar.activation(out=pl[:, 0, :], in_=xs, func=ACT.Relu, scale=-1.0 / H, bias=XI[1] / H)
+            nc.scalar.activation(out=pl[:, 4, :], in_=xs, func=ACT.Relu, scale=1.0 / H, bias=-XI[4] / H)
+            nc.scalar.activation(out=fn[:, 0, :], in_=pl[:, 0, :], func=ACT.Square, scale=A, bias=0.0)
+            nc.scalar.activation(out=fn[:, 1, :], in_=pl[:, 0, :], func=ACT.Square, scale=-A, bias=A)
+            nc.scalar.activation(out=fn[:, 5, :], in_=pl[:, 4, :], func=ACT.Square, scale=A, bias=0.0)
+            nc.scalar.activation(out=fb[:, 3, :], in_=pl[:, 4, :], func=ACT.Square, scale=-A, bias=A)
 
         def func_s_tail(t):
             pl, fn, fb = pls[t], fns[t], fbs[t]
@@ -211,16 +213,17 @@ def tile_kanlayer_t_kernel(tc, x, base_weight, spline_weight, grad_out, out):
             j, bc = t // 4, t % 4
             bank = psum.tile([P, 512], F32, tag="mx", name="bank")
             banks[q] = bank
-            if p < 6:
-                mx(bank, j, bc, 0, p + 2, True, False)
-                mx(bank, j, bc, 1, p + 1, False, False)
-                mx(bank, j, bc, 0, p, False, True)
-            elif p == 6:
+            if p == 4:
                 mx(bank, j, bc, 0, 2, True, False)
                 mx(bank, j, bc, 0, 2, False, False)
                 mx(bank, j, bc, 1, 0, False, True)
-            else:
+            elif p == 7:
                 mx(bank, j, bc, 0, L, True, True)
+            else:
+                m = p if p < 4 else p - 1
+                mx(bank, j, bc, 0, m + 2, True, False)
+                mx(bank, j, bc, 1, m + 1, False, False)
+                mx(bank, j, bc, 0, m, False, True)
 
         def consume(q):
             t, p = q // NPLANES, q % NPLANES
@@ -230,25 +233,27 @@ def tile_kanlayer_t_kernel(tc, x, base_weight, spline_weight, grad_out, out):
                 nc.vector.scalar_tensor_tensor(
                     out=fn[:, 0, :], in0=fn[:, 0, :], scalar=-1.25, in1=bank[:], op0=ALU.add, op1=ALU.mult
                 )
-            elif p < 5:
+            elif p < 4 or p == 5:
+                a = p if p < 4 else 4
                 nc.vector.scalar_tensor_tensor(
-                    out=fn[:, p, :], in0=fn[:, p, :], scalar=1.25, in1=bank[:], op0=ALU.add, op1=ALU.mult
+                    out=fn[:, a, :], in0=fn[:, a, :], scalar=1.25, in1=bank[:], op0=ALU.add, op1=ALU.mult
                 )
-            elif p == 5:
-                nc.vector.tensor_tensor(out=fn[:, 5, :], in0=fn[:, 5, :], in1=bank[:], op=ALU.mult)
             elif p == 6:
+                nc.vector.tensor_tensor(out=fn[:, 5, :], in0=fn[:, 5, :], in1=bank[:], op=ALU.mult)
+            elif p == 4:
                 nc.vector.scalar_tensor_tensor(
                     out=fn[:, 0, :], in0=bank[:], scalar=0.625, in1=fn[:, 0, :], op0=ALU.mult, op1=ALU.subtract
                 )
+                nc.vector.tensor_tensor(out=fn[:, 0:2, :], in0=fn[:, 0:2, :], in1=fn[:, 2:4, :], op=ALU.add)
             else:
-                nc.vector.tensor_tensor(out=fn[:, 1, :], in0=fn[:, 1, :], in1=bank[:], op=ALU.add)
+                nc.vector.tensor_tensor(out=fn[:, 4, :], in0=fn[:, 4, :], in1=bank[:], op=ALU.add)
 
         def adder(t):
             fn = fns[t]
             ob = aux.tile([P, 4, P], F32, tag="aux", name="ob")
             obs[t] = ob
             for r in range(4):
-                for a in range(6):
+                for a in (0, 1, 4, 5):
                     nc.tensor.matmul(
                         out=ob[:, r, :],
                         lhsT=fn[:, a, P * r : P * r + P],

@@ -167,7 +167,7 @@ def tile_kanlayer_t_kernel(tc, x, base_weight, spline_weight, grad_out, out):
             pl = plp.tile([P, 5, 512], F32, name="pl")
             pls[t] = pl
             for k in range(1, 4):
-                nc.vector.tensor_scalar(
+                nc.gpsimd.tensor_scalar(
                     out=pl[:, k, :], in0=xs, scalar1=XI[k], scalar2=XI[k + 1], op0=ALU.max, op1=ALU.min
                 )
 

from contextlib import ExitStack

import concourse.mybir as mybir
from concourse.masks import make_identity

F32 = mybir.dt.float32
BF16 = mybir.dt.bfloat16
U32 = mybir.dt.uint32
U8 = mybir.dt.uint8
E4X4 = mybir.dt.float8_e4m3fn_x4
E5X4 = mybir.dt.float8_e5m2_x4
ALU = mybir.AluOpType
ACT = mybir.ActivationFunctionType

P = 128
B, I, O, L = 2048, 512, 512, 8
FLOPS = 2 * B * O * (I + I * L)

H = 0.4
XI = [-1.0 + H * k for k in range(6)]
A = 1.25 ** 0.5
S = A / H
NTILES = 16
NPLANES = 8
LEAD = 6


def tile_kanlayer_t_kernel(tc, x, base_weight, spline_weight, grad_out, out):
    nc = tc.nc
    with ExitStack() as ctx:
        keep = ctx.enter_context(tc.tile_pool(name="keep", bufs=1))
        grp = ctx.enter_context(tc.tile_pool(name="grp", bufs=2))
        plp = ctx.enter_context(tc.tile_pool(name="plp", bufs=2))
        fnp = ctx.enter_context(tc.tile_pool(name="fnp", bufs=3))
        fbp = ctx.enter_context(tc.tile_pool(name="fbp", bufs=2))
        outp = ctx.enter_context(tc.tile_pool(name="outp", bufs=3))
        psum = ctx.enter_context(tc.psum_pool(name="psum", bufs=LEAD))
        aux = ctx.enter_context(tc.psum_pool(name="aux", bufs=2))
        ctx.enter_context(tc.manual_schedule())

        ident = keep.tile([P, P], F32)
        make_identity(nc, ident[:])
        ident_bf = keep.tile([P, P], BF16)
        make_identity(nc, ident_bf[:])
        w_codes = keep.tile([P, 4, L, P], U32, align_bytes=64)
        w_scales = keep.tile([P, 4, L, P], U8, align_bytes=64)
        wb_codes = keep.tile([P, I], U32, align_bytes=64)
        wb_scales = keep.tile([P, I], U8, align_bytes=64)
        g_codes = keep.tile([P, 2, B], U32, align_bytes=64)
        g_scales = keep.tile([P, 2, B], U8, align_bytes=64)
        xT = keep.tile([P, 4, B], BF16)
        x_sb = keep.tile([P, 16, I], BF16)
        g_sb = keep.tile([P, 16, O], BF16)
        w_raw = keep.tile([P, 4, 4, L * P], BF16)
        wb_raw = keep.tile([P, 4, I], BF16)
        wg = keep.tile([P, L, P, 4], BF16, align_bytes=64)

        g_view = grad_out.rearrange("(n p) o -> p n o", p=P)
        x_view = x.rearrange("(n p) i -> p n i", p=P)
        sw = spline_weight.rearrange("o i l -> o (i l)")

        def load_g(bc):
            nc.sync.dma_start(out=g_sb[:, 4 * bc : 4 * bc + 4, :], in_=g_view[:, 4 * bc : 4 * bc + 4, :])

        def load_x(bc):
            nc.sync.dma_start(out=x_sb[:, 4 * bc : 4 * bc + 4, :], in_=x_view[:, 4 * bc : 4 * bc + 4, :])

        def load_w(j):
            for u in range(2):
                nc.sync.dma_start(
                    out=w_raw[:, j, 2 * u : 2 * u + 2, :],
                    in_=sw[256 * u : 256 * u + 256, L * P * j : L * P * (j + 1)].rearrange("(q e) c -> q e c", e=2),
                )

        load_x(0)
        load_g(0)
        load_w(0)
        load_g(1)
        load_x(1)
        for u in range(2):
            nc.sync.dma_start(
                out=wb_raw[:, 2 * u : 2 * u + 2, :],
                in_=base_weight[256 * u : 256 * u + 256, :].rearrange("(q e) c -> q e c", e=2),
            )
        for bc in range(2, 4):
            load_g(bc)
            load_x(bc)
        for j in range(1, 4):
            load_w(j)

        ggs = {}
        xts = {}
        xps = {}

        def g_transpose(bc, c2):
            xt = aux.tile([P, 2, 2, P], F32, tag="aux", name="xt")
            xts[(bc, c2)] = xt
            for n2 in range(2):
                gw = g_sb[:, 4 * bc + 2 * c2 + n2, :].bitcast(F32)
                for u in range(2):
                    nc.tensor.transpose(xt[:, n2, u, :], gw[:, P * u : P * u + P], ident[:])

        def g_copy(bc, c2, on_vector):
            if c2 == 0:
                ggs[bc] = grp.tile([P, 512, 4], BF16, align_bytes=64, tag="gg", name="gg")
            ggf = ggs[bc][:].rearrange("p b t -> p (b t)").bitcast(F32).rearrange("p (b u) -> p b u", u=2)
            dst = ggf[:, 256 * c2 : 256 * c2 + 256, :].rearrange("p (n b) u -> p n b u", n=2)
            src = xts[(bc, c2)][:].rearrange("p n u b -> p n b u")
            if on_vector:
                nc.vector.tensor_copy(out=dst, in_=src)
            else:
                nc.scalar.copy(out=dst, in_=src)

        def g_quantise(bc):
            gg2 = grp.tile([P, 512, 4], BF16, align_bytes=64, tag="gg2", name="gg2")
            flat = ggs[bc][:].rearrange("p b t -> p (b t)")
            flat2 = gg2[:].rearrange("p b t -> p (b t)")
            nc.vector.tensor_scalar(out=flat2, in0=flat, scalar1=-2.0, scalar2=None, op0=ALU.mult)
            cols = slice(512 * bc, 512 * bc + 512)
            nc.vector.quantize_mx(out=g_codes[:, 0, cols].bitcast(E5X4), scales=g_scales[:, 0, cols], in_=flat)
            nc.vector.quantize_mx(out=g_codes[:, 1, cols].bitcast(E5X4), scales=g_scales[:, 1, cols], in_=flat2)

        def x_transpose(bc, j2):
            xp = aux.tile([P, 2, 512], BF16, tag="aux", name="xp")
            xps[(bc, j2)] = xp
            for jj in range(2):
                j = 2 * j2 + jj
                for q in range(4):
                    nc.tensor.transpose(
                        xp[:, jj, P * q : P * q + P], x_sb[:, 4 * bc + q, P * j : P * j + P], ident_bf[:]
                    )

        def x_copy(bc, j2):
            nc.scalar.copy(out=xT[:, 2 * j2 : 2 * j2 + 2, 512 * bc : 512 * bc + 512], in_=xps[(bc, j2)][:])

        def w_regroup(j, on_vector):
            src = w_raw[:, j].rearrange("p t (i l) -> p l i t", l=L)
            cut = 4 if j == 0 else 2
            if on_vector:
                nc.vector.tensor_copy(out=wg[:, 0:cut], in_=src[:, 0:cut])
            else:
                nc.scalar.copy(out=wg[:, cut:L], in_=src[:, cut:L])

        def w_quantise(j):
            nc.vector.quantize_mx(
                out=w_codes[:, j].rearrange("p l i -> p (l i)").bitcast(E4X4),
                scales=w_scales[:, j].rearrange("p l i -> p (l i)"),
                in_=wg[:].rearrange("p l i t -> p (l i t)"),
            )

        def pre_base():
            wbg = grp.tile([P, 512, 4], BF16, align_bytes=64, tag="gg", name="wbg")
            nc.scalar.copy(out=wbg[:], in_=wb_raw[:].rearrange("p t i -> p i t"))
            nc.vector.quantize_mx(
                out=wb_codes[:].bitcast(E4X4), scales=wb_scales[:], in_=wbg[:].rearrange("p i t -> p (i t)")
            )

        fns = {}
        fbs = {}
        pls = {}
        banks = {}
        obs = {}

        def func_v(t):
            j, bc = t // 4, t % 4
            xs = xT[:, j, 512 * bc : 512 * bc + 512]
            pl = plp.tile([P, 5, 512], F32, name="pl")
            pls[t] = pl
            for k in range(1, 4):
                nc.gpsimd.tensor_scalar(
                    out=pl[:, k, :], in0=xs, scalar1=XI[k], scalar2=XI[k + 1], op0=ALU.max, op1=ALU.min
                )

        def func_s_head(t):
            j, bc = t // 4, t % 4
            xs = xT[:, j, 512 * bc : 512 * bc + 512]
            pl = pls[t]
            fn = fnp.tile([P, 6, 512], F32, name="fn")
            fb = fbp.tile([P, 4, 512], F32, name="fb")
            fns[t] = fn
            fbs[t] = fb
            nc.scalar.activation(out=pl[:, 0, :], in_=xs, func=ACT.Relu, scale=-1.0 / H, bias=XI[1] / H)
            nc.scalar.activation(out=pl[:, 4, :], in_=xs, func=ACT.Relu, scale=1.0 / H, bias=-XI[4] / H)
            nc.scalar.activation(out=fn[:, 0, :], in_=pl[:, 0, :], func=ACT.Square, scale=A, bias=0.0)
            nc.scalar.activation(out=fn[:, 1, :], in_=pl[:, 0, :], func=ACT.Square, scale=-A, bias=A)
            nc.scalar.activation(out=fn[:, 5, :], in_=pl[:, 4, :], func=ACT.Square, scale=A, bias=0.0)
            nc.scalar.activation(out=fb[:, 3, :], in_=pl[:, 4, :], func=ACT.Square, scale=-A, bias=A)

        def func_s_tail(t):
            pl, fn, fb = pls[t], fns[t], fbs[t]
            for k in range(1, 4):
                nc.scalar.activation(out=fn[:, k + 1, :], in_=pl[:, k, :], func=ACT.Square, scale=S, bias=-S * XI[k])
                nc.scalar.activation(out=fb[:, k - 1, :], in_=pl[:, k, :], func=ACT.Square, scale=-S, bias=S * XI[k + 1])

        def mx(bank, j, bc, v, l, start, stop):
            gc = slice(512 * bc, 512 * bc + 512)
            if l < L:
                lhsT, lhsT_scale = w_codes[:, j, l, :], w_scales[:, j, l, :]
            else:
                lhsT, lhsT_scale = wb_codes[:, P * j : P * j + P], wb_scales[:, P * j : P * j + P]
            nc.tensor.matmul_mx(
                out=bank[:],
                lhsT=lhsT.bitcast(E4X4),
                lhsT_scale=lhsT_scale,
                rhs=g_codes[:, v, gc].bitcast(E5X4),
                rhs_scale=g_scales[:, v, gc],
                start=start,
                stop=stop,
            )

        def issue_mx(q):
            t, p = q // NPLANES, q % NPLANES
            j, bc = t // 4, t % 4
            bank = psum.tile([P, 512], F32, tag="mx", name="bank")
            banks[q] = bank
            if p == 4:
                mx(bank, j, bc, 0, 2, True, False)
                mx(bank, j, bc, 0, 2, False, False)
                mx(bank, j, bc, 1, 0, False, True)
            elif p == 7:
                mx(bank, j, bc, 0, L, True, True)
            else:
                m = p if p < 4 else p - 1
                mx(bank, j, bc, 0, m + 2, True, False)
                mx(bank, j, bc, 1, m + 1, False, False)
                mx(bank, j, bc, 0, m, False, True)

        def consume(q):
            t, p = q // NPLANES, q % NPLANES
            fn = fns[t]
            bank = banks[q]
            if p == 0:
                nc.vector.scalar_tensor_tensor(
                    out=fn[:, 0, :], in0=fn[:, 0, :], scalar=-1.25, in1=bank[:], op0=ALU.add, op1=ALU.mult
                )
            elif p < 4 or p == 5:
                a = p if p < 4 else 4
                nc.vector.scalar_tensor_tensor(
                    out=fn[:, a, :], in0=fn[:, a, :], scalar=1.25, in1=bank[:], op0=ALU.add, op1=ALU.mult
                )
            elif p == 6:
                nc.vector.tensor_tensor(out=fn[:, 5, :], in0=fn[:, 5, :], in1=bank[:], op=ALU.mult)
            elif p == 4:
                nc.vector.scalar_tensor_tensor(
                    out=fn[:, 0, :], in0=bank[:], scalar=0.625, in1=fn[:, 0, :], op0=ALU.mult, op1=ALU.subtract
                )
                nc.vector.tensor_tensor(out=fn[:, 0:2, :], in0=fn[:, 0:2, :], in1=fn[:, 2:4, :], op=ALU.add)
            else:
                nc.vector.tensor_tensor(out=fn[:, 4, :], in0=fn[:, 4, :], in1=bank[:], op=ALU.add)

        def adder(t):
            fn = fns[t]
            ob = aux.tile([P, 4, P], F32, tag="aux", name="ob")
            obs[t] = ob
            for r in range(4):
                for a in (0, 1, 4, 5):
                    nc.tensor.matmul(
                        out=ob[:, r, :],
                        lhsT=fn[:, a, P * r : P * r + P],
                        rhs=ident[:],
                        is_transpose=True,
                        start=(a == 0),
                        stop=(a == 5),
                    )

        def finish(t):
            j, bc = t // 4, t % 4
            ot = outp.tile([P, 4, P], F32, name="ot")
            nc.scalar.copy(out=ot[:], in_=obs[t][:])
            nc.sync.dma_start(
                out=out[512 * bc : 512 * bc + 512, P * j : P * j + P].rearrange("(r p) i -> p r i", p=P), in_=ot[:]
            )

        x_transpose(0, 0)
        x_copy(0, 0)
        g_transpose(0, 0)
        g_transpose(0, 1)
        g_copy(0, 0, False)
        g_copy(0, 1, False)
        func_v(0)
        func_s_head(0)
        g_quantise(0)
        w_regroup(0, True)
        w_regroup(0, False)
        x_transpose(1, 0)
        g_transpose(1, 0)
        g_copy(1, 0, True)
        g_transpose(1, 1)
        g_copy(1, 1, True)
        w_quantise(0)
        func_s_tail(0)
        x_copy(1, 0)
        for q in range(LEAD):
            issue_mx(q)
        g_quantise(1)
        pre_base()
        for t in range(NTILES):
            if t + 1 < NTILES:
                func_v(t + 1)
                func_s_head(t + 1)
                func_s_tail(t + 1)
            if t >= 1:
                finish(t - 1)
            if t + 2 < 4:
                x_transpose(t + 2, 0)
                g_transpose(t + 2, 0)
                x_copy(t + 2, 0)
                g_transpose(t + 2, 1)
                g_copy(t + 2, 0, False)
                g_copy(t + 2, 1, False)
            if 2 <= t < 6:
                x_transpose(t - 2, 1)
                x_copy(t - 2, 1)
            if t % 4 == 1 and t // 4 + 1 < 4:
                w_regroup(t // 4 + 1, False)
            if 2 <= t + 1 < 4:
                g_quantise(t + 1)
            if t % 4 == 2 and t // 4 + 1 < 4:
                w_regroup(t // 4 + 1, True)
                w_quantise(t // 4 + 1)
            nc.vector.tensor_tensor(out=fns[t][:, 1:5, :], in0=fns[t][:, 1:5, :], in1=fbs[t][:], op=ALU.subtract)
            for p in range(NPLANES):
                q = NPLANES * t + p
                consume(q)
                if q + LEAD < NPLANES * NTILES:
                    issue_mx(q + LEAD)
            adder(t)
        finish(NTILES - 1)
